import numpy as np
import ml_dtypes


def mxq(x, axis, fmt="e4m3"):
    dtype, down = {"e4m3": (ml_dtypes.float8_e4m3fn, 7), "e5m2": (ml_dtypes.float8_e5m2, 14)}[fmt]
    v = np.moveaxis(np.asarray(x, np.float32).astype(ml_dtypes.bfloat16).astype(np.float64), axis, -1)
    blocks = v.reshape(v.shape[:-1] + (-1, 32))
    amax = np.abs(blocks).max(-1, keepdims=True)
    byte = np.maximum(np.where(amax > 0, np.frexp(amax)[1] - 1 + 127, 0) - down, 1)
    scale = np.exp2(byte - 127.0)
    codes = (blocks / scale).astype(np.float32).astype(dtype).astype(np.float64)
    return np.moveaxis((codes * scale).reshape(v.shape), -1, axis)


WIDE = False


def mx_kscale(k):
    if not WIDE:
        return np.ones(k)
    levels = np.array([10, -10, 5, -5, 0])
    if k % 512:
        return np.exp2(np.random.permutation(np.resize(levels, k // 32))).repeat(32)
    a = np.empty((k // 512, 16))
    for p in range(k // 512):
        a[p, :8] = np.random.permutation(np.resize(levels, 8))
        for g in range(8):
            far = levels[np.abs(levels - a[p, g]) >= 10]
            a[p, g + 8] = far[np.random.randint(len(far))]
    return np.exp2(a.ravel()).repeat(32)


BF16 = ml_dtypes.bfloat16


def bf(x):
    return np.asarray(x, np.float32).astype(BF16)


def f64(x):
    return np.asarray(x).astype(np.float64)


B, EMBED, DETER, STOC, HID, ACT = 4096, 512, 512, 64, 512, 12
DIST = 2 * STOC
CAT = DETER + EMBED


def softplus(v):
    return np.maximum(v, 0.0) + np.log(1.0 + np.exp(-np.abs(v)))


def draw0():
    s = mx_kscale(CAT)
    tp, tq = mx_kscale(HID), mx_kscale(HID)
    r = np.random.standard_normal
    return {
        "h": bf(r((B, DETER)) * 0.65 * s[:DETER]),
        "embedding": bf(r((B, EMBED)) * s[DETER:]),
        "wp1": bf(r((HID, DETER)) / np.sqrt(DETER) / s[:DETER] * tp[:, None]),
        "bp1": bf(r(HID) * 0.1 * tp),
        "wp2": bf(r((DIST, HID)) / np.sqrt(HID) / tp),
        "bp2": bf(r(DIST) * 0.1),
        "wq1": bf(r((HID, CAT)) / np.sqrt(CAT) / s * tq[:, None]),
        "bq1": bf(r(HID) * 0.1 * tq),
        "wq2": bf(r((DIST, HID)) / np.sqrt(HID) / tq),
        "bq2": bf(r(DIST) * 0.1),
    }


def core(h, embedding, wp1, bp1, wp2, bp2, wq1, bq1, wq2, bq2):
    cq = mxq(np.concatenate([f64(h), f64(embedding)], -1), 1, "e4m3")
    ap = np.maximum((cq[:, :DETER] @ mxq(f64(wp1), 1, "e4m3").T) + f64(bp1), 0.0)
    prior = (mxq(ap, 1, "e4m3") @ mxq(f64(wp2), 1, "e4m3").T) + f64(bp2)
    prior_mean, prior_std = np.split(prior, 2, axis=-1)
    prior_std = softplus(prior_std) + 0.1
    aq = np.maximum((cq @ mxq(f64(wq1), 1, "e4m3").T) + f64(bq1), 0.0)
    post = (mxq(aq, 1, "e4m3") @ mxq(f64(wq2), 1, "e4m3").T) + f64(bq2)
    post_mean, post_std = np.split(post, 2, axis=-1)
    post_std = softplus(post_std) + 0.1
    return (post_mean, post_std, prior_mean, prior_std)


def e4m3fn_bytes(y):
    return np.clip(np.asarray(y, np.float64), -448.0, 448.0).astype(np.float32).astype(ml_dtypes.float8_e4m3fn).view(np.uint8)


def e4m3fn_values(b):
    return np.asarray(b, np.uint8).view(ml_dtypes.float8_e4m3fn).astype(np.float64)


def setup_inputs():
    d = draw0()
    x0 = np.asarray(d['h']).astype(np.float64)
    s = (np.max(np.abs(x0), axis=(0,), keepdims=True) / 448.0).astype(np.float32)
    out = {}
    for k, v in d.items():
        if k == 'h':
            out['h_bytes'] = e4m3fn_bytes(x0 / s.astype(np.float64))
            out['h_scale'] = s
        else:
            out[k] = v
    return out


def reference(h_bytes, h_scale, embedding, wp1, bp1, wp2, bp2, wq1, bq1, wq2, bq2):
    return core(e4m3fn_values(h_bytes) * h_scale.astype(np.float64), embedding, wp1, bp1, wp2, bp2, wq1, bq1, wq2, bq2)

@@ -1,0 +1,291 @@
+from contextlib import ExitStack
+
+import concourse.mybir as mybir
+from concourse.masks import make_identity
+
+B, KIN, HID, DIST, LAT = 4096, 512, 512, 128, 64
+FLOPS = 2 * B * (HID * KIN + HID * 2 * KIN + 2 * DIST * HID)
+
+P = 128
+J = 4
+TOK = P * J
+CHUNKS = B // TOK
+
+F32 = mybir.dt.float32
+BF16 = mybir.dt.bfloat16
+U32 = mybir.dt.uint32
+U8 = mybir.dt.uint8
+FP8 = mybir.dt.float8_e4m3fn
+FP8X4 = mybir.dt.float8_e4m3fn_x4
+ACT = mybir.ActivationFunctionType
+ALU = mybir.AluOpType
+ENG = mybir.EngineType
+
+PRIOR, POST = 0, 1
+HEADS = (PRIOR, POST)
+
+
+def tile_rssmcell_pb_t_kernel(
+    tc, h_bytes, h_scale, embedding, wp1, bp1, wp2, bp2, wq1, bq1, wq2, bq2,
+    post_mean, post_std, prior_mean, prior_std,
+):
+    nc = tc.nc
+    with ExitStack() as ctx:
+        keep = ctx.enter_context(tc.tile_pool(name="keep", bufs=1))
+        work = ctx.enter_context(tc.tile_pool(name="work", bufs=2))
+        psum = ctx.enter_context(tc.psum_pool(name="psum", bufs=1))
+
+        srow = keep.tile([P, KIN], F32, name="srow", tag="srow")
+        brow = keep.tile([P, 2 * DIST], BF16, name="brow", tag="brow")
+        ones = keep.tile([P, P], F32, name="ones", tag="ones")
+        ones_b = keep.tile([P, P], BF16, name="ones_b", tag="ones_b")
+        ident = keep.tile([P, P], F32, name="ident", tag="ident")
+        warm = keep.tile([P, 1], F32, name="warm", tag="warm")
+        b1r = [keep.tile([P, 4], BF16, name="b1r_%d" % e, tag="b1r_%d" % e) for e in HEADS]
+        b1 = [keep.tile([P, 4], F32, name="b1_%d" % e, tag="b1_%d" % e) for e in HEADS]
+        b2 = keep.tile([P, 2, 2, LAT], F32, name="b2", tag="b2")
+        scale = keep.tile([P, KIN], F32, name="scale", tag="scale", align_bytes=64)
+        neg = keep.tile([P, 1], F32, name="neg", tag="neg")
+        wp1r = keep.tile([P, 4, KIN], BF16, name="wp1r", tag="wp1r")
+        wq1r = keep.tile([P, 4, 2 * KIN], BF16, name="wq1r", tag="wq1r")
+        w2r = keep.tile([P, 2, HID], BF16, name="w2r", tag="w2r")
+        w1g = keep.tile([P, 3, HID, 4], BF16, name="w1g", tag="w1g", align_bytes=64)
+        w1c = keep.tile([P, 3, HID], U32, name="w1c", tag="w1c", align_bytes=64)
+        w1s = keep.tile([P, 3, HID], U8, name="w1s", tag="w1s", align_bytes=64)
+        w2g = keep.tile([P, 2, DIST, 4], BF16, name="w2g", tag="w2g", align_bytes=64)
+        w2c = keep.tile([P, 2, DIST], U32, name="w2c", tag="w2c", align_bytes=64)
+        w2s = keep.tile([P, 2, DIST], U8, name="w2s", tag="w2s", align_bytes=64)
+
+        hby, emb, hb, cg, cc, cs = {}, {}, {}, {}, {}, {}
+        pl, ag, ac, asc, v, y, mm2 = {}, {}, {}, {}, {}, {}, {}
+
+        def load(i):
+            hby[i] = work.tile([P, J, KIN], U8, name="hby", tag="hby", bufs=5, align_bytes=64)
+            nc.sync.dma_start(out=hby[i][:], in_=h_bytes.rearrange("(c p j) k -> c p j k", p=P, j=J)[i])
+            emb[i] = work.tile([P, J, KIN], BF16, name="emb", tag="emb", bufs=5)
+            nc.sync.dma_start(out=emb[i][:], in_=embedding.rearrange("(c p j) k -> c p j k", p=P, j=J)[i])
+
+        def widen(i):
+            hb[i] = work.tile([P, J, KIN], BF16, name="hb", tag="hb", bufs=2, align_bytes=64)
+            for j in range(J):
+                nc.vector.tensor_tensor(
+                    out=hb[i][:, j, :], in0=hby[i][:, j, :].bitcast(FP8), in1=scale[:], op=ALU.mult)
+
+        def turn(i, j):
+            xt = psum.tile([P, 2, 2, P], F32, name="xt", tag="xt", bufs=2)
+            for g, src in enumerate((hb[i], emb[i])):
+                words = src[:, j, :].bitcast(F32)
+                for u in (0, 1):
+                    nc.tensor.transpose(xt[:, g, u, :], words[:, u : KIN // 2 : 2], ident[:])
+            return xt
+
+        def unload(i, j, xt):
+            if j == 0:
+                cg[i] = work.tile([P, 2, TOK, 4], BF16, name="cg", tag="cg", bufs=2, align_bytes=64)
+            dst = cg[i][:, :, j * P : (j + 1) * P, :].bitcast(F32)
+            nc.scalar.copy(out=dst, in_=xt[:].rearrange("p g u r -> p g r u"))
+
+        def quant_c(i):
+            cc[i] = work.tile([P, 2, TOK], U32, name="cc", tag="cc", bufs=2, align_bytes=64)
+            cs[i] = work.tile([P, 2, TOK], U8, name="cs", tag="cs", bufs=2, align_bytes=64)
+            for g in (0, 1):
+                nc.vector.quantize_mx(
+                    out=cc[i][:, g, :].bitcast(FP8X4), scales=cs[i][:, g, :],
+                    in_=cg[i][:, g, :, :].rearrange("p n t -> p (n t)"))
+
+        def first(i, head):
+            pl[i, head] = work.tile([P, 4, TOK], BF16, name="pl", tag="pl", bufs=3, align_bytes=64)
+            passes = [(0, 0)] if head == PRIOR else [(1, 0), (2, 1)]
+            for t in range(4):
+                acc = psum.tile([P, TOK], F32, name="acc", tag="acc", bufs=4)
+                cols = slice(t * P, (t + 1) * P)
+                for n, (w, g) in enumerate(passes):
+                    nc.tensor.matmul_mx(
+                        out=acc[:], lhsT=w1c[:, w, cols].bitcast(FP8X4), lhsT_scale=w1s[:, w, cols],
+                        rhs=cc[i][:, g, :].bitcast(FP8X4), rhs_scale=cs[i][:, g, :],
+                        start=(n == 0), stop=(n == len(passes) - 1))
+                nc.scalar.activation(out=pl[i, head][:, t, :], in_=acc[:], func=ACT.Relu, bias=b1[head][:, t : t + 1])
+
+        def interleave(i, head):
+            ag[i, head] = work.tile([P, TOK, 4], BF16, name="ag", tag="ag", bufs=3, align_bytes=64)
+            nc.vector.tensor_copy(
+                out=ag[i, head][:].rearrange("p (c i) t -> p c t i", i=4),
+                in_=pl[i, head][:].rearrange("p t (c i) -> p c t i", i=4))
+
+        def quant_a(i, head):
+            ac[i, head] = work.tile([P, TOK], U32, name="ac", tag="ac", bufs=3, align_bytes=64)
+            asc[i, head] = work.tile([P, TOK], U8, name="asc", tag="asc", bufs=3, align_bytes=64)
+            nc.vector.quantize_mx(
+                out=ac[i, head][:].bitcast(FP8X4), scales=asc[i, head][:],
+                in_=ag[i, head][:].rearrange("p n t -> p (n t)"))
+
+        def second(i, head):
+            o = psum.tile([P, J, 2, LAT], F32, name="o%d" % head, tag="o%d" % head, bufs=1)
+            mm2[i, head] = o
+            for j in range(J):
+                cols = slice(j * P, (j + 1) * P)
+                nc.tensor.matmul_mx(
+                    out=o[:, j, :, :].rearrange("p h c -> p (h c)"),
+                    lhsT=ac[i, head][:, cols].bitcast(FP8X4), lhsT_scale=asc[i, head][:, cols],
+                    rhs=w2c[:, head, :].bitcast(FP8X4), rhs_scale=w2s[:, head, :], start=True, stop=True)
+
+        def bias(i, head):
+            if head == PRIOR:
+                v[i] = work.tile([P, 2, 2, J, LAT], F32, name="v", tag="v", bufs=8)
+            nc.vector.tensor_tensor(
+                out=v[i][:, head].rearrange("p h j c -> p j h c"),
+                in0=mm2[i, head][:],
+                in1=b2[:, head].unsqueeze(1).to_broadcast([P, J, 2, LAT]),
+                op=ALU.add)
+            dst = prior_mean if head == PRIOR else post_mean
+            nc.sync.dma_start(
+                out=dst.rearrange("(c p j) d -> c p j d", p=P, j=J)[i], in_=v[i][:, head, 0])
+
+        def exp(i, heads=slice(0, 2)):
+            if i not in y:
+                y[i] = work.tile([P, 2, J * LAT], F32, name="y", tag="y", bufs=8)
+            t = y[i][:, heads]
+            nc.scalar.activation(
+                out=t, in_=v[i][:, heads, 1].rearrange("p e j c -> p e (j c)"), func=ACT.Abs, bias=neg[:])
+            nc.scalar.activation(out=t, in_=t, func=ACT.Exp, scale=-1.0)
+
+        def log(i):
+            nc.scalar.activation(out=y[i][:], in_=y[i][:], func=ACT.Ln, bias=1.0)
+
+        def std(i):
+            sd = v[i][:, :, 1].rearrange("p e j c -> p e (j c)")
+            nc.vector.scalar_tensor_tensor(out=sd, in0=sd, scalar=0.1, in1=y[i][:], op0=ALU.max, op1=ALU.add)
+            for head in HEADS:
+                dst = prior_std if head == PRIOR else post_std
+                nc.sync.dma_start(
+                    out=dst.rearrange("(c p j) d -> c p j d", p=P, j=J)[i], in_=v[i][:, head, 1])
+
+        def turn_weights(src, k0, t0):
+            xt = psum.tile([P, 2, 2, P], F32, name="xt", tag="xt", bufs=2)
+            for a in (0, 1):
+                words = src[:, t0 + a, k0 : k0 + KIN].bitcast(F32)
+                for u in (0, 1):
+                    nc.tensor.transpose(xt[:, a, u, :], words[:, u : KIN // 2 : 2], ident[:])
+            return xt
+
+        def weight_dst(w, t0):
+            return w1g[:, w, t0 * P : (t0 + 2) * P, :].rearrange("p (a m) e -> p a m e", a=2).bitcast(F32)
+
+        def quant_w(w):
+            nc.vector.quantize_mx(
+                out=w1c[:, w, :].bitcast(FP8X4), scales=w1s[:, w, :],
+                in_=w1g[:, w].rearrange("p m t -> p (m t)"))
+
+        nc.vector.memset(srow[:], 0.0)
+        nc.vector.memset(ones[:], 1.0)
+        nc.vector.memset(warm[:], 0.0)
+        nc.vector.tensor_scalar(out=neg[:], in0=warm[:], scalar1=-0.1, scalar2=None, op0=ALU.add)
+        nc.vector.memset(ones_b[:], 1.0)
+        nc.vector.memset(brow[:], 0.0)
+        make_identity(nc, ident[:])
+        nc.scalar.activation(out=warm[:], in_=warm[:], func=ACT.Exp)
+
+        nc.sync.dma_start(out=srow[0:1, :], in_=h_scale)
+        load(0)
+        nc.sync.dma_start(out=wp1r[:], in_=wp1.rearrange("(m t) k -> m t k", t=4))
+        nc.sync.dma_start(out=wq1r[:], in_=wq1.rearrange("(m t) k -> m t k", t=4))
+        nc.scalar.dma_start(out=b1r[PRIOR][:], in_=bp1.rearrange("(m t) -> m t", t=4))
+        nc.scalar.dma_start(out=b1r[POST][:], in_=bq1.rearrange("(m t) -> m t", t=4))
+        load(1)
+        nc.sync.dma_start(out=w2r[:, PRIOR, :], in_=wp2)
+        nc.sync.dma_start(out=w2r[:, POST, :], in_=wq2)
+        nc.sync.dma_start(out=brow[0:1, 0:DIST], in_=bp2.unsqueeze(0))
+        nc.sync.dma_start(out=brow[0:1, DIST : 2 * DIST], in_=bq2.unsqueeze(0))
+        load(2)
+        load(3)
+
+        with tc.manual_schedule(engines={ENG.PE, ENG.Activation, ENG.DVE}):
+            sp = psum.tile([P, KIN], F32, name="o0", tag="o0", bufs=1)
+            nc.tensor.matmul(out=sp[:], lhsT=ones[:], rhs=srow[:], start=True, stop=True)
+            nc.scalar.copy(out=scale[:], in_=sp[:])
+            widen(0)
+            for t0 in (0, 2):
+                x = turn_weights(wp1r, 0, t0)
+                nc.scalar.copy(out=weight_dst(0, t0), in_=x[:].rearrange("p a u m -> p a m u"))
+            quant_w(0)
+            for j in range(J):
+                unload(0, j, turn(0, j))
+            for head in HEADS:
+                nc.vector.tensor_copy(out=b1[head][:], in_=b1r[head][:])
+            quant_c(0)
+            widen(1)
+            for w in (1, 2):
+                for t0 in (0, 2):
+                    x = turn_weights(wq1r, (w - 1) * KIN, t0)
+                    nc.scalar.copy(out=weight_dst(w, t0), in_=x[:].rearrange("p a u m -> p a m u"))
+                quant_w(w)
+            xt = psum.tile([P, 2, 2, P], F32, name="xt", tag="xt", bufs=2)
+            for head in HEADS:
+                words = w2r[:, head, :].bitcast(F32)
+                for u in (0, 1):
+                    nc.tensor.transpose(xt[:, head, u, :], words[:, u : KIN // 2 : 2], ident[:])
+            nc.scalar.copy(out=w2g[:].bitcast(F32), in_=xt[:].rearrange("p a u m -> p a m u"))
+            bp = psum.tile([P, 2, 2, LAT], F32, name="o1", tag="o1", bufs=1)
+            nc.tensor.matmul(out=bp[:].rearrange("p e h c -> p (e h c)"), lhsT=ones_b[:], rhs=brow[:], start=True, stop=True)
+
+            for i in range(CHUNKS - 1):
+                if i + 4 < CHUNKS:
+                    load(i + 4)
+                for j in (0, 1):
+                    unload(i + 1, j, turn(i + 1, j))
+                if 0 < i:
+                    interleave(i - 1, POST)
+                first(i, PRIOR)
+                if 2 <= i:
+                    exp(i - 2)
+                for j in (2, 3):
+                    unload(i + 1, j, turn(i + 1, j))
+                if i + 2 < CHUNKS:
+                    widen(i + 2)
+                if 0 < i:
+                    quant_a(i - 1, POST)
+                first(i, POST)
+                interleave(i, PRIOR)
+                quant_c(i + 1)
+                quant_a(i, PRIOR)
+                if i == 0:
+                    nc.vector.quantize_mx(
+                        out=w2c[:].rearrange("p e m -> p (e m)").bitcast(FP8X4),
+                        scales=w2s[:].rearrange("p e m -> p (e m)"),
+                        in_=w2g[:].rearrange("p e m t -> p (e m t)"))
+                    nc.vector.tensor_copy(out=b2[:, :, 0], in_=bp[:, :, 0])
+                    nc.vector.tensor_scalar(out=b2[:, :, 1], in0=bp[:, :, 1], scalar1=0.1, scalar2=None, op0=ALU.add)
+                if 0 < i < CHUNKS - 2:
+                    second(i - 1, PRIOR)
+                    second(i - 1, POST)
+                    bias(i - 1, PRIOR)
+                    bias(i - 1, POST)
+
+            i = CHUNKS - 1
+            first(i, PRIOR)
+            second(i - 2, PRIOR)
+            second(i - 2, POST)
+            interleave(i - 1, POST)
+            bias(i - 2, PRIOR)
+            bias(i - 2, POST)
+            quant_a(i - 1, POST)
+            first(i, POST)
+            exp(i - 2)
+            interleave(i, PRIOR)
+            second(i - 1, PRIOR)
+            second(i - 1, POST)
+            quant_a(i, PRIOR)
+            bias(i - 1, PRIOR)
+            bias(i - 1, POST)
+            exp(i - 1)
+            interleave(i, POST)
+            second(i, PRIOR)
+            bias(i, PRIOR)
+            exp(i, slice(0, 1))
+            quant_a(i, POST)
+            second(i, POST)
+            bias(i, POST)
+            exp(i, slice(1, 2))
+            for c in range(CHUNKS):
+                log(c)
+                std(c)

@@ -1,3 +1,4 @@
+import math
 from contextlib import ExitStack
 
 import concourse.mybir as mybir
@@ -21,6 +22,7 @@ ACT = mybir.ActivationFunctionType
 ALU = mybir.AluOpType
 ENG = mybir.EngineType
 
+LIMIT = 40.0
 PRIOR, POST = 0, 1
 HEADS = (PRIOR, POST)
 
@@ -45,7 +47,7 @@ def tile_rssmcell_pb_t_kernel(
         b1 = [keep.tile([P, 4], F32, name="b1_%d" % e, tag="b1_%d" % e) for e in HEADS]
         b2 = keep.tile([P, 2, 2, LAT], F32, name="b2", tag="b2")
         scale = keep.tile([P, KIN], F32, name="scale", tag="scale", align_bytes=64)
-        neg = keep.tile([P, 1], F32, name="neg", tag="neg")
+        off = keep.tile([P, 1], F32, name="off", tag="off")
         wp1r = keep.tile([P, 4, KIN], BF16, name="wp1r", tag="wp1r")
         wq1r = keep.tile([P, 4, 2 * KIN], BF16, name="wq1r", tag="wq1r")
         w2r = keep.tile([P, 2, HID], BF16, name="w2r", tag="w2r")
@@ -59,14 +61,16 @@ def tile_rssmcell_pb_t_kernel(
         hby, emb, hb, cg, cc, cs = {}, {}, {}, {}, {}, {}
         pl, ag, ac, asc, v, y, mm2 = {}, {}, {}, {}, {}, {}, {}
 
-        def load(i):
+        def load_h(i):
             hby[i] = work.tile([P, J, KIN], U8, name="hby", tag="hby", bufs=5, align_bytes=64)
             nc.sync.dma_start(out=hby[i][:], in_=h_bytes.rearrange("(c p j) k -> c p j k", p=P, j=J)[i])
+
+        def load_e(i):
             emb[i] = work.tile([P, J, KIN], BF16, name="emb", tag="emb", bufs=5)
             nc.sync.dma_start(out=emb[i][:], in_=embedding.rearrange("(c p j) k -> c p j k", p=P, j=J)[i])
 
         def widen(i):
-            hb[i] = work.tile([P, J, KIN], BF16, name="hb", tag="hb", bufs=2, align_bytes=64)
+            hb[i] = work.tile([P, J, KIN], BF16, name="hb", tag="hb", bufs=3, align_bytes=64)
             for j in range(J):
                 nc.vector.tensor_tensor(
                     out=hb[i][:, j, :], in0=hby[i][:, j, :].bitcast(FP8), in1=scale[:], op=ALU.mult)
@@ -86,8 +90,8 @@ def tile_rssmcell_pb_t_kernel(
             nc.scalar.copy(out=dst, in_=xt[:].rearrange("p g u r -> p g r u"))
 
         def quant_c(i):
-            cc[i] = work.tile([P, 2, TOK], U32, name="cc", tag="cc", bufs=2, align_bytes=64)
-            cs[i] = work.tile([P, 2, TOK], U8, name="cs", tag="cs", bufs=2, align_bytes=64)
+            cc[i] = work.tile([P, 2, TOK], U32, name="cc", tag="cc", bufs=3, align_bytes=64)
+            cs[i] = work.tile([P, 2, TOK], U8, name="cs", tag="cs", bufs=3, align_bytes=64)
             for g in (0, 1):
                 nc.vector.quantize_mx(
                     out=cc[i][:, g, :].bitcast(FP8X4), scales=cs[i][:, g, :],
@@ -113,8 +117,8 @@ def tile_rssmcell_pb_t_kernel(
                 in_=pl[i, head][:].rearrange("p t (c i) -> p c t i", i=4))
 
         def quant_a(i, head):
-            ac[i, head] = work.tile([P, TOK], U32, name="ac", tag="ac", bufs=3, align_bytes=64)
-            asc[i, head] = work.tile([P, TOK], U8, name="asc", tag="asc", bufs=3, align_bytes=64)
+            ac[i, head] = work.tile([P, TOK], U32, name="ac", tag="ac", bufs=4, align_bytes=64)
+            asc[i, head] = work.tile([P, TOK], U8, name="asc", tag="asc", bufs=4, align_bytes=64)
             nc.vector.quantize_mx(
                 out=ac[i, head][:].bitcast(FP8X4), scales=asc[i, head][:],
                 in_=ag[i, head][:].rearrange("p n t -> p (n t)"))
@@ -144,17 +148,15 @@ def tile_rssmcell_pb_t_kernel(
         def exp(i, heads=slice(0, 2)):
             if i not in y:
                 y[i] = work.tile([P, 2, J * LAT], F32, name="y", tag="y", bufs=8)
-            t = y[i][:, heads]
             nc.scalar.activation(
-                out=t, in_=v[i][:, heads, 1].rearrange("p e j c -> p e (j c)"), func=ACT.Abs, bias=neg[:])
-            nc.scalar.activation(out=t, in_=t, func=ACT.Exp, scale=-1.0)
+                out=y[i][:, heads], in_=v[i][:, heads, 1].rearrange("p e j c -> p e (j c)"), func=ACT.Exp)
 
         def log(i):
-            nc.scalar.activation(out=y[i][:], in_=y[i][:], func=ACT.Ln, bias=1.0)
+            nc.scalar.activation(out=y[i][:], in_=y[i][:], func=ACT.Ln, bias=off[:])
 
         def std(i):
             sd = v[i][:, :, 1].rearrange("p e j c -> p e (j c)")
-            nc.vector.scalar_tensor_tensor(out=sd, in0=sd, scalar=0.1, in1=y[i][:], op0=ALU.max, op1=ALU.add)
+            nc.vector.scalar_tensor_tensor(out=sd, in0=y[i][:], scalar=LIMIT, in1=sd, op0=ALU.min, op1=ALU.max)
             for head in HEADS:
                 dst = prior_std if head == PRIOR else post_std
                 nc.sync.dma_start(
@@ -179,75 +181,102 @@ def tile_rssmcell_pb_t_kernel(
         nc.vector.memset(srow[:], 0.0)
         nc.vector.memset(ones[:], 1.0)
         nc.vector.memset(warm[:], 0.0)
-        nc.vector.tensor_scalar(out=neg[:], in0=warm[:], scalar1=-0.1, scalar2=None, op0=ALU.add)
+        nc.vector.tensor_scalar(out=off[:], in0=warm[:], scalar1=math.exp(0.1), scalar2=None, op0=ALU.add)
         nc.vector.memset(ones_b[:], 1.0)
         nc.vector.memset(brow[:], 0.0)
         make_identity(nc, ident[:])
         nc.scalar.activation(out=warm[:], in_=warm[:], func=ACT.Exp)
 
         nc.sync.dma_start(out=srow[0:1, :], in_=h_scale)
-        load(0)
-        nc.sync.dma_start(out=wp1r[:], in_=wp1.rearrange("(m t) k -> m t k", t=4))
-        nc.sync.dma_start(out=wq1r[:], in_=wq1.rearrange("(m t) k -> m t k", t=4))
         nc.scalar.dma_start(out=b1r[PRIOR][:], in_=bp1.rearrange("(m t) -> m t", t=4))
         nc.scalar.dma_start(out=b1r[POST][:], in_=bq1.rearrange("(m t) -> m t", t=4))
-        load(1)
+        nc.sync.dma_start(out=wp1r[:], in_=wp1.rearrange("(m t) k -> m t k", t=4))
+        load_h(0)
+        load_e(0)
+        load_h(1)
+        nc.sync.dma_start(out=wq1r[:], in_=wq1.rearrange("(m t) k -> m t k", t=4))
+        load_e(1)
+        load_h(2)
         nc.sync.dma_start(out=w2r[:, PRIOR, :], in_=wp2)
         nc.sync.dma_start(out=w2r[:, POST, :], in_=wq2)
         nc.sync.dma_start(out=brow[0:1, 0:DIST], in_=bp2.unsqueeze(0))
         nc.sync.dma_start(out=brow[0:1, DIST : 2 * DIST], in_=bq2.unsqueeze(0))
-        load(2)
-        load(3)
+        load_e(2)
+        load_h(3)
+        load_e(3)
 
         with tc.manual_schedule(engines={ENG.PE, ENG.Activation, ENG.DVE}):
             sp = psum.tile([P, KIN], F32, name="o0", tag="o0", bufs=1)
             nc.tensor.matmul(out=sp[:], lhsT=ones[:], rhs=srow[:], start=True, stop=True)
             nc.scalar.copy(out=scale[:], in_=sp[:])
+            x = turn_weights(wp1r, 0, 0)
+            nc.vector.tensor_copy(out=weight_dst(0, 0), in_=x[:].rearrange("p a u m -> p a m u"))
+            x = turn_weights(wp1r, 0, 2)
+            nc.vector.tensor_copy(out=weight_dst(0, 2), in_=x[:].rearrange("p a u m -> p a m u"))
             widen(0)
-            for t0 in (0, 2):
-                x = turn_weights(wp1r, 0, t0)
-                nc.scalar.copy(out=weight_dst(0, t0), in_=x[:].rearrange("p a u m -> p a m u"))
             quant_w(0)
             for j in range(J):
                 unload(0, j, turn(0, j))
+            widen(1)
             for head in HEADS:
                 nc.vector.tensor_copy(out=b1[head][:], in_=b1r[head][:])
             quant_c(0)
-            widen(1)
-            for w in (1, 2):
-                for t0 in (0, 2):
-                    x = turn_weights(wq1r, (w - 1) * KIN, t0)
-                    nc.scalar.copy(out=weight_dst(w, t0), in_=x[:].rearrange("p a u m -> p a m u"))
-                quant_w(w)
-            xt = psum.tile([P, 2, 2, P], F32, name="xt", tag="xt", bufs=2)
+            x = turn_weights(wq1r, 0, 0)
+            nc.scalar.copy(out=weight_dst(1, 0), in_=x[:].rearrange("p a u m -> p a m u"))
+            x = turn_weights(wq1r, 0, 2)
+            nc.scalar.copy(out=weight_dst(1, 2), in_=x[:].rearrange("p a u m -> p a m u"))
+            quant_w(1)
+            x = turn_weights(wq1r, 512, 0)
+            nc.scalar.copy(out=weight_dst(2, 0), in_=x[:].rearrange("p a u m -> p a m u"))
+            x = turn_weights(wq1r, 512, 2)
+            nc.scalar.copy(out=weight_dst(2, 2), in_=x[:].rearrange("p a u m -> p a m u"))
+            quant_w(2)
+            x = psum.tile([P, 2, 2, P], F32, name="xt", tag="xt", bufs=2)
             for head in HEADS:
                 words = w2r[:, head, :].bitcast(F32)
                 for u in (0, 1):
-                    nc.tensor.transpose(xt[:, head, u, :], words[:, u : KIN // 2 : 2], ident[:])
-            nc.scalar.copy(out=w2g[:].bitcast(F32), in_=xt[:].rearrange("p a u m -> p a m u"))
+                    nc.tensor.transpose(x[:, head, u, :], words[:, u : KIN // 2 : 2], ident[:])
+            nc.scalar.copy(out=w2g[:].bitcast(F32), in_=x[:].rearrange("p a u m -> p a m u"))
             bp = psum.tile([P, 2, 2, LAT], F32, name="o1", tag="o1", bufs=1)
             nc.tensor.matmul(out=bp[:].rearrange("p e h c -> p (e h c)"), lhsT=ones_b[:], rhs=brow[:], start=True, stop=True)
 
-            for i in range(CHUNKS - 1):
-                if i + 4 < CHUNKS:
-                    load(i + 4)
-                for j in (0, 1):
-                    unload(i + 1, j, turn(i + 1, j))
-                if 0 < i:
+            def has(c):
+                return 0 <= c < CHUNKS
+
+            for i in range(-1, CHUNKS - 1):
+                n = i + 2
+                if has(n + 3) and n + 3 > 3:
+                    load_h(n + 3)
+                    load_e(n + 3)
+                if has(n):
+                    for j in (0, 1):
+                        unload(n, j, turn(n, j))
+                if has(i - 1):
                     interleave(i - 1, POST)
-                first(i, PRIOR)
-                if 2 <= i:
-                    exp(i - 2)
-                for j in (2, 3):
-                    unload(i + 1, j, turn(i + 1, j))
-                if i + 2 < CHUNKS:
-                    widen(i + 2)
-                if 0 < i:
+                if has(i):
+                    first(i, PRIOR)
+                if has(i - 2):
+                    second(i - 2, PRIOR)
+                    second(i - 2, POST)
+                if has(i - 3):
+                    exp(i - 3)
+                if has(n):
+                    for j in (2, 3):
+                        unload(n, j, turn(n, j))
+                if has(n + 1):
+                    widen(n + 1)
+                if has(i - 1):
                     quant_a(i - 1, POST)
-                first(i, POST)
-                interleave(i, PRIOR)
-                quant_c(i + 1)
-                quant_a(i, PRIOR)
+                if has(i - 2):
+                    bias(i - 2, PRIOR)
+                    bias(i - 2, POST)
+                if has(i):
+                    first(i, POST)
+                    interleave(i, PRIOR)
+                if has(n):
+                    quant_c(n)
+                if has(i):
+                    quant_a(i, PRIOR)
                 if i == 0:
                     nc.vector.quantize_mx(
                         out=w2c[:].rearrange("p e m -> p (e m)").bitcast(FP8X4),
@@ -255,22 +284,20 @@ def tile_rssmcell_pb_t_kernel(
                         in_=w2g[:].rearrange("p e m t -> p (e m t)"))
                     nc.vector.tensor_copy(out=b2[:, :, 0], in_=bp[:, :, 0])
                     nc.vector.tensor_scalar(out=b2[:, :, 1], in0=bp[:, :, 1], scalar1=0.1, scalar2=None, op0=ALU.add)
-                if 0 < i < CHUNKS - 2:
-                    second(i - 1, PRIOR)
-                    second(i - 1, POST)
-                    bias(i - 1, PRIOR)
-                    bias(i - 1, POST)
 
             i = CHUNKS - 1
             first(i, PRIOR)
             second(i - 2, PRIOR)
             second(i - 2, POST)
+            exp(i - 3)
             interleave(i - 1, POST)
             bias(i - 2, PRIOR)
             bias(i - 2, POST)
             quant_a(i - 1, POST)
             first(i, POST)
             exp(i - 2)
+            for c in range(i - 1):
+                log(c)
             interleave(i, PRIOR)
             second(i - 1, PRIOR)
             second(i - 1, POST)
@@ -283,9 +310,12 @@ def tile_rssmcell_pb_t_kernel(
             bias(i, PRIOR)
             exp(i, slice(0, 1))
             quant_a(i, POST)
-            second(i, POST)
-            bias(i, POST)
-            exp(i, slice(1, 2))
-            for c in range(CHUNKS):
+            for c in range(i - 1):
+                std(c)
+                if c == 0:
+                    second(i, POST)
+                    bias(i, POST)
+                    exp(i, slice(1, 2))
+            for c in (i - 1, i):
                 log(c)
                 std(c)

@@ -23,6 +23,7 @@ ALU = mybir.AluOpType
 ENG = mybir.EngineType
 
 LIMIT = 40.0
+ON_V = {(0, 0, 0), (7, 1, 3), (0, 0, 2)}
 PRIOR, POST = 0, 1
 HEADS = (PRIOR, POST)
 
@@ -108,7 +109,11 @@ def tile_rssmcell_pb_t_kernel(
                         out=acc[:], lhsT=w1c[:, w, cols].bitcast(FP8X4), lhsT_scale=w1s[:, w, cols],
                         rhs=cc[i][:, g, :].bitcast(FP8X4), rhs_scale=cs[i][:, g, :],
                         start=(n == 0), stop=(n == len(passes) - 1))
-                nc.scalar.activation(out=pl[i, head][:, t, :], in_=acc[:], func=ACT.Relu, bias=b1[head][:, t : t + 1])
+                if (i, head, t) in ON_V:
+                    nc.vector.tensor_scalar(
+                        out=pl[i, head][:, t, :], in0=acc[:], scalar1=b1[head][:, t : t + 1], scalar2=0.0, op0=ALU.add, op1=ALU.max)
+                else:
+                    nc.scalar.activation(out=pl[i, head][:, t, :], in_=acc[:], func=ACT.Relu, bias=b1[head][:, t : t + 1])
 
         def interleave(i, head):
             ag[i, head] = work.tile([P, TOK, 4], BF16, name="ag", tag="ag", bufs=3, align_bytes=64)
@@ -162,6 +167,10 @@ def tile_rssmcell_pb_t_kernel(
                 nc.sync.dma_start(
                     out=dst.rearrange("(c p j) d -> c p j d", p=P, j=J)[i], in_=v[i][:, head, 1])
 
+        def spin(count):
+            for n in range(count):
+                nc.tensor.matmul(out=junk[:], lhsT=ones[:], rhs=ones[:], start=True, stop=True)
+
         def turn_weights(src, k0, t0):
             xt = psum.tile([P, 2, 2, P], F32, name="xt", tag="xt", bufs=2)
             for a in (0, 1):
@@ -179,7 +188,7 @@ def tile_rssmcell_pb_t_kernel(
                 in_=w1g[:, w].rearrange("p m t -> p (m t)"))
 
         nc.vector.memset(srow[:], 0.0)
-        nc.vector.memset(ones[:], 1.0)
+        nc.gpsimd.memset(ones[:], 1.0)
         nc.vector.memset(warm[:], 0.0)
         nc.vector.tensor_scalar(out=off[:], in0=warm[:], scalar1=math.exp(0.1), scalar2=None, op0=ALU.add)
         nc.vector.memset(ones_b[:], 1.0)
@@ -204,33 +213,64 @@ def tile_rssmcell_pb_t_kernel(
         load_e(2)
         load_h(3)
         load_e(3)
+        load_h(4)
+        load_e(4)
 
         with tc.manual_schedule(engines={ENG.PE, ENG.Activation, ENG.DVE}):
+            junk = psum.tile([P, P], F32, name="o1", tag="o1", bufs=1)
+            spin(5)
             sp = psum.tile([P, KIN], F32, name="o0", tag="o0", bufs=1)
             nc.tensor.matmul(out=sp[:], lhsT=ones[:], rhs=srow[:], start=True, stop=True)
             nc.scalar.copy(out=scale[:], in_=sp[:])
             x = turn_weights(wp1r, 0, 0)
-            nc.vector.tensor_copy(out=weight_dst(0, 0), in_=x[:].rearrange("p a u m -> p a m u"))
+            nc.scalar.copy(out=weight_dst(0, 0), in_=x[:].rearrange("p a u m -> p a m u"))
             x = turn_weights(wp1r, 0, 2)
-            nc.vector.tensor_copy(out=weight_dst(0, 2), in_=x[:].rearrange("p a u m -> p a m u"))
+            nc.scalar.copy(out=weight_dst(0, 2), in_=x[:].rearrange("p a u m -> p a m u"))
             widen(0)
+            spin(2)
             quant_w(0)
-            for j in range(J):
-                unload(0, j, turn(0, j))
+            unload(0, 0, turn(0, 0))
+            unload(0, 1, turn(0, 1))
+            spin(2)
+            unload(0, 2, turn(0, 2))
+            unload(0, 3, turn(0, 3))
+            load_h(5)
+            load_e(5)
             widen(1)
             for head in HEADS:
                 nc.vector.tensor_copy(out=b1[head][:], in_=b1r[head][:])
-            quant_c(0)
+            spin(2)
             x = turn_weights(wq1r, 0, 0)
             nc.scalar.copy(out=weight_dst(1, 0), in_=x[:].rearrange("p a u m -> p a m u"))
             x = turn_weights(wq1r, 0, 2)
             nc.scalar.copy(out=weight_dst(1, 2), in_=x[:].rearrange("p a u m -> p a m u"))
+            quant_c(0)
+            spin(1)
             quant_w(1)
-            x = turn_weights(wq1r, 512, 0)
-            nc.scalar.copy(out=weight_dst(2, 0), in_=x[:].rearrange("p a u m -> p a m u"))
             x = turn_weights(wq1r, 512, 2)
             nc.scalar.copy(out=weight_dst(2, 2), in_=x[:].rearrange("p a u m -> p a m u"))
+            first(0, PRIOR)
+            x = turn_weights(wq1r, 512, 0)
+            nc.vector.tensor_copy(out=weight_dst(2, 0), in_=x[:].rearrange("p a u m -> p a m u"))
+            unload(1, 0, turn(1, 0))
+            unload(1, 1, turn(1, 1))
+            unload(1, 2, turn(1, 2))
+            spin(2)
+            unload(1, 3, turn(1, 3))
+            widen(2)
             quant_w(2)
+            first(0, POST)
+            interleave(0, PRIOR)
+            widen(3)
+            quant_a(0, PRIOR)
+            quant_c(1)
+            unload(2, 0, turn(2, 0))
+            unload(2, 1, turn(2, 1))
+            spin(1)
+            unload(2, 2, turn(2, 2))
+            unload(2, 3, turn(2, 3))
+            quant_c(2)
+            spin(2)
             x = psum.tile([P, 2, 2, P], F32, name="xt", tag="xt", bufs=2)
             for head in HEADS:
                 words = w2r[:, head, :].bitcast(F32)
@@ -239,11 +279,17 @@ def tile_rssmcell_pb_t_kernel(
             nc.scalar.copy(out=w2g[:].bitcast(F32), in_=x[:].rearrange("p a u m -> p a m u"))
             bp = psum.tile([P, 2, 2, LAT], F32, name="o1", tag="o1", bufs=1)
             nc.tensor.matmul(out=bp[:].rearrange("p e h c -> p (e h c)"), lhsT=ones_b[:], rhs=brow[:], start=True, stop=True)
+            nc.vector.quantize_mx(
+                out=w2c[:].rearrange("p e m -> p (e m)").bitcast(FP8X4),
+                scales=w2s[:].rearrange("p e m -> p (e m)"),
+                in_=w2g[:].rearrange("p e m t -> p (e m t)"))
+            nc.vector.tensor_copy(out=b2[:, :, 0], in_=bp[:, :, 0])
+            nc.vector.tensor_scalar(out=b2[:, :, 1], in0=bp[:, :, 1], scalar1=0.1, scalar2=None, op0=ALU.add)
 
             def has(c):
                 return 0 <= c < CHUNKS
 
-            for i in range(-1, CHUNKS - 1):
+            for i in range(1, CHUNKS - 1):
                 n = i + 2
                 if has(n + 3) and n + 3 > 3:
                     load_h(n + 3)
@@ -277,13 +323,6 @@ def tile_rssmcell_pb_t_kernel(
                     quant_c(n)
                 if has(i):
                     quant_a(i, PRIOR)
-                if i == 0:
-                    nc.vector.quantize_mx(
-                        out=w2c[:].rearrange("p e m -> p (e m)").bitcast(FP8X4),
-                        scales=w2s[:].rearrange("p e m -> p (e m)"),
-                        in_=w2g[:].rearrange("p e m t -> p (e m t)"))
-                    nc.vector.tensor_copy(out=b2[:, :, 0], in_=bp[:, :, 0])
-                    nc.vector.tensor_scalar(out=b2[:, :, 1], in0=bp[:, :, 1], scalar1=0.1, scalar2=None, op0=ALU.add)
 
             i = CHUNKS - 1
             first(i, PRIOR)

@@ -9,8 +9,9 @@ FLOPS = 2 * B * (HID * KIN + HID * 2 * KIN + 2 * DIST * HID)
 
 P = 128
 J = 4
-TOK = P * J
-CHUNKS = B // TOK
+PACK = 4
+CHUNK = P * J
+CHUNKS = B // CHUNK
 
 F32 = mybir.dt.float32
 BF16 = mybir.dt.bfloat16
@@ -22,10 +23,11 @@ ACT = mybir.ActivationFunctionType
 ALU = mybir.AluOpType
 ENG = mybir.EngineType
 
-LIMIT = 40.0
-ON_V = {(0, 0, 0), (7, 1, 3), (0, 0, 2)}
+EXACT_ABOVE = 40.0
 PRIOR, POST = 0, 1
 HEADS = (PRIOR, POST)
+MEAN, STD = 0, 1
+PASSES = {PRIOR: ((0, 0),), POST: ((1, 0), (2, 1))}
 
 
 def tile_rssmcell_pb_t_kernel(
@@ -38,323 +40,326 @@ def tile_rssmcell_pb_t_kernel(
         work = ctx.enter_context(tc.tile_pool(name="work", bufs=2))
         psum = ctx.enter_context(tc.psum_pool(name="psum", bufs=1))
 
-        srow = keep.tile([P, KIN], F32, name="srow", tag="srow")
-        brow = keep.tile([P, 2 * DIST], BF16, name="brow", tag="brow")
+        scale_row = keep.tile([P, KIN], F32, name="scale_row", tag="scale_row")
+        bias2_row = keep.tile([P, 2 * DIST], BF16, name="bias2_row", tag="bias2_row")
         ones = keep.tile([P, P], F32, name="ones", tag="ones")
-        ones_b = keep.tile([P, P], BF16, name="ones_b", tag="ones_b")
+        ones_bf16 = keep.tile([P, P], BF16, name="ones_bf16", tag="ones_bf16")
         ident = keep.tile([P, P], F32, name="ident", tag="ident")
-        warm = keep.tile([P, 1], F32, name="warm", tag="warm")
-        b1r = [keep.tile([P, 4], BF16, name="b1r_%d" % e, tag="b1r_%d" % e) for e in HEADS]
-        b1 = [keep.tile([P, 4], F32, name="b1_%d" % e, tag="b1_%d" % e) for e in HEADS]
-        b2 = keep.tile([P, 2, 2, LAT], F32, name="b2", tag="b2")
-        scale = keep.tile([P, KIN], F32, name="scale", tag="scale", align_bytes=64)
-        off = keep.tile([P, 1], F32, name="off", tag="off")
-        wp1r = keep.tile([P, 4, KIN], BF16, name="wp1r", tag="wp1r")
-        wq1r = keep.tile([P, 4, 2 * KIN], BF16, name="wq1r", tag="wq1r")
-        w2r = keep.tile([P, 2, HID], BF16, name="w2r", tag="w2r")
-        w1g = keep.tile([P, 3, HID, 4], BF16, name="w1g", tag="w1g", align_bytes=64)
-        w1c = keep.tile([P, 3, HID], U32, name="w1c", tag="w1c", align_bytes=64)
-        w1s = keep.tile([P, 3, HID], U8, name="w1s", tag="w1s", align_bytes=64)
-        w2g = keep.tile([P, 2, DIST, 4], BF16, name="w2g", tag="w2g", align_bytes=64)
-        w2c = keep.tile([P, 2, DIST], U32, name="w2c", tag="w2c", align_bytes=64)
-        w2s = keep.tile([P, 2, DIST], U8, name="w2s", tag="w2s", align_bytes=64)
+        zero = keep.tile([P, 1], F32, name="zero", tag="zero")
+        bias1_raw = [keep.tile([P, PACK], BF16, name="bias1_raw_%d" % e, tag="bias1_raw_%d" % e) for e in HEADS]
+        bias1 = [keep.tile([P, PACK], F32, name="bias1_%d" % e, tag="bias1_%d" % e) for e in HEADS]
+        bias2 = keep.tile([P, 2, 2, LAT], F32, name="bias2", tag="bias2")
+        scale = keep.tile([P, 2, KIN], F32, name="scale", tag="scale", align_bytes=64)
+        exp_tenth = keep.tile([P, 1], F32, name="exp_tenth", tag="exp_tenth")
+        wp1_rows = keep.tile([P, PACK, KIN], BF16, name="wp1_rows", tag="wp1_rows")
+        wq1_rows = keep.tile([P, PACK, 2 * KIN], BF16, name="wq1_rows", tag="wq1_rows")
+        w2_rows = keep.tile([P, 2, HID], BF16, name="w2_rows", tag="w2_rows")
+        value = keep.tile([P, 2 * CHUNKS, 2, J, LAT], F32, name="value", tag="value")
+        soft = keep.tile([P, 2 * CHUNKS, J * LAT], F32, name="soft", tag="soft")
+        w1_grouped = keep.tile([P, 3, HID, PACK], BF16, name="w1_grouped", tag="w1_grouped", align_bytes=64)
+        w1_codes = keep.tile([P, 3, HID], U32, name="w1_codes", tag="w1_codes", align_bytes=64)
+        w1_scales = keep.tile([P, 3, HID], U8, name="w1_scales", tag="w1_scales", align_bytes=64)
+        w2_grouped = keep.tile([P, 2, DIST, PACK], BF16, name="w2_grouped", tag="w2_grouped", align_bytes=64)
+        w2_codes = keep.tile([P, 2, DIST], U32, name="w2_codes", tag="w2_codes", align_bytes=64)
+        w2_scales = keep.tile([P, 2, DIST], U8, name="w2_scales", tag="w2_scales", align_bytes=64)
 
-        hby, emb, hb, cg, cc, cs = {}, {}, {}, {}, {}, {}
-        pl, ag, ac, asc, v, y, mm2 = {}, {}, {}, {}, {}, {}, {}
+        h_raw, emb, h_wide, c_grouped, c_codes, c_scales = {}, {}, {}, {}, {}, {}
+        planes, a_grouped, a_codes, a_scales, result = {}, {}, {}, {}, {}
+
+
+        def turn_weights(rows, k0, t0):
+            bank = psum.tile([P, 2, 2, P], F32, name="turned", tag="turned", bufs=2)
+            for a in (0, 1):
+                words = rows[:, t0 + a, k0 : k0 + KIN].bitcast(F32)
+                for u in (0, 1):
+                    nc.tensor.transpose(bank[:, a, u, :], words[:, u : KIN // 2 : 2], ident[:])
+            return bank
+
+        def unload_weights(copy, w, t0, bank):
+            dst = w1_grouped[:, w, t0 * P : (t0 + 2) * P, :].rearrange("p (a m) e -> p a m e", a=2).bitcast(F32)
+            copy(out=dst, in_=bank[:].rearrange("p a u m -> p a m u"))
+
+        def quantise_weights(w):
+            nc.vector.quantize_mx(
+                out=w1_codes[:, w, :].bitcast(FP8X4), scales=w1_scales[:, w, :],
+                in_=w1_grouped[:, w].rearrange("p m t -> p (m t)"))
+
+        def filler(count):
+            for n in range(count):
+                nc.tensor.matmul(out=unread[:], lhsT=ones[:], rhs=ones[:], start=True, stop=True)
+
 
         def load_h(i):
-            hby[i] = work.tile([P, J, KIN], U8, name="hby", tag="hby", bufs=5, align_bytes=64)
-            nc.sync.dma_start(out=hby[i][:], in_=h_bytes.rearrange("(c p j) k -> c p j k", p=P, j=J)[i])
+            h_raw[i] = work.tile([P, J, KIN], U8, name="h_raw", tag="h_raw", bufs=5, align_bytes=64)
+            nc.sync.dma_start(out=h_raw[i][:], in_=h_bytes.rearrange("(c p j) k -> c p j k", p=P, j=J)[i])
 
-        def load_e(i):
+        def load_embedding(i):
             emb[i] = work.tile([P, J, KIN], BF16, name="emb", tag="emb", bufs=5)
             nc.sync.dma_start(out=emb[i][:], in_=embedding.rearrange("(c p j) k -> c p j k", p=P, j=J)[i])
 
         def widen(i):
-            hb[i] = work.tile([P, J, KIN], BF16, name="hb", tag="hb", bufs=3, align_bytes=64)
-            for j in range(J):
+            h_wide[i] = work.tile([P, J, KIN], BF16, name="h_wide", tag="h_wide", bufs=3, align_bytes=64)
+            step = 1 if i < 2 else 2
+            for j in range(0, J, step):
+                rows = slice(j, j + step)
                 nc.vector.tensor_tensor(
-                    out=hb[i][:, j, :], in0=hby[i][:, j, :].bitcast(FP8), in1=scale[:], op=ALU.mult)
+                    out=h_wide[i][:, rows].rearrange("p j k -> p (j k)"),
+                    in0=h_raw[i][:, rows].rearrange("p j k -> p (j k)").bitcast(FP8),
+                    in1=scale[:, 0:step].rearrange("p j k -> p (j k)"), op=ALU.mult)
 
         def turn(i, j):
-            xt = psum.tile([P, 2, 2, P], F32, name="xt", tag="xt", bufs=2)
-            for g, src in enumerate((hb[i], emb[i])):
-                words = src[:, j, :].bitcast(F32)
+            bank = psum.tile([P, 2, 2, P], F32, name="turned", tag="turned", bufs=2)
+            for g, rows in enumerate((h_wide[i], emb[i])):
+                words = rows[:, j, :].bitcast(F32)
                 for u in (0, 1):
-                    nc.tensor.transpose(xt[:, g, u, :], words[:, u : KIN // 2 : 2], ident[:])
-            return xt
-
-        def unload(i, j, xt):
+                    nc.tensor.transpose(bank[:, g, u, :], words[:, u : KIN // 2 : 2], ident[:])
             if j == 0:
-                cg[i] = work.tile([P, 2, TOK, 4], BF16, name="cg", tag="cg", bufs=2, align_bytes=64)
-            dst = cg[i][:, :, j * P : (j + 1) * P, :].bitcast(F32)
-            nc.scalar.copy(out=dst, in_=xt[:].rearrange("p g u r -> p g r u"))
+                c_grouped[i] = work.tile([P, 2, CHUNK, PACK], BF16, name="c_grouped", tag="c_grouped", bufs=2, align_bytes=64)
+            dst = c_grouped[i][:, :, j * P : (j + 1) * P, :].bitcast(F32)
+            nc.scalar.copy(out=dst, in_=bank[:].rearrange("p g u r -> p g r u"))
 
-        def quant_c(i):
-            cc[i] = work.tile([P, 2, TOK], U32, name="cc", tag="cc", bufs=3, align_bytes=64)
-            cs[i] = work.tile([P, 2, TOK], U8, name="cs", tag="cs", bufs=3, align_bytes=64)
-            for g in (0, 1):
+        def quantise_c(i):
+            c_codes[i] = work.tile([P, 2, CHUNK], U32, name="c_codes", tag="c_codes", bufs=3, align_bytes=64)
+            c_scales[i] = work.tile([P, 2, CHUNK], U8, name="c_scales", tag="c_scales", bufs=3, align_bytes=64)
+            step = 1 if i == 0 else 2
+            for g in range(0, 2, step):
+                part = slice(g, g + step)
                 nc.vector.quantize_mx(
-                    out=cc[i][:, g, :].bitcast(FP8X4), scales=cs[i][:, g, :],
-                    in_=cg[i][:, g, :, :].rearrange("p n t -> p (n t)"))
+                    out=c_codes[i][:, part].rearrange("p g n -> p (g n)").bitcast(FP8X4),
+                    scales=c_scales[i][:, part].rearrange("p g n -> p (g n)"),
+                    in_=c_grouped[i][:, part].rearrange("p g n t -> p (g n t)"))
+
 
         def first(i, head):
-            pl[i, head] = work.tile([P, 4, TOK], BF16, name="pl", tag="pl", bufs=3, align_bytes=64)
-            passes = [(0, 0)] if head == PRIOR else [(1, 0), (2, 1)]
-            for t in range(4):
-                acc = psum.tile([P, TOK], F32, name="acc", tag="acc", bufs=4)
+            planes[i, head] = work.tile([P, PACK, CHUNK], BF16, name="planes", tag="planes", bufs=3, align_bytes=64)
+            passes = PASSES[head]
+            for t in range(PACK):
+                acc = psum.tile([P, CHUNK], F32, name="acc", tag="acc", bufs=4)
                 cols = slice(t * P, (t + 1) * P)
                 for n, (w, g) in enumerate(passes):
                     nc.tensor.matmul_mx(
-                        out=acc[:], lhsT=w1c[:, w, cols].bitcast(FP8X4), lhsT_scale=w1s[:, w, cols],
-                        rhs=cc[i][:, g, :].bitcast(FP8X4), rhs_scale=cs[i][:, g, :],
+                        out=acc[:], lhsT=w1_codes[:, w, cols].bitcast(FP8X4), lhsT_scale=w1_scales[:, w, cols],
+                        rhs=c_codes[i][:, g, :].bitcast(FP8X4), rhs_scale=c_scales[i][:, g, :],
                         start=(n == 0), stop=(n == len(passes) - 1))
-                if (i, head, t) in ON_V:
-                    nc.vector.tensor_scalar(
-                        out=pl[i, head][:, t, :], in0=acc[:], scalar1=b1[head][:, t : t + 1], scalar2=0.0, op0=ALU.add, op1=ALU.max)
+                dst = planes[i, head][:, t, :]
+                bias = bias1[head][:, t : t + 1]
+                if (i, head, t) == (0, PRIOR, 2):
+                    nc.vector.tensor_scalar(out=dst, in0=acc[:], scalar1=bias, scalar2=0.0, op0=ALU.add, op1=ALU.max)
                 else:
-                    nc.scalar.activation(out=pl[i, head][:, t, :], in_=acc[:], func=ACT.Relu, bias=b1[head][:, t : t + 1])
+                    nc.scalar.activation(out=dst, in_=acc[:], func=ACT.Relu, bias=bias)
 
         def interleave(i, head):
-            ag[i, head] = work.tile([P, TOK, 4], BF16, name="ag", tag="ag", bufs=3, align_bytes=64)
+            a_grouped[i, head] = work.tile([P, CHUNK, PACK], BF16, name="a_grouped", tag="a_grouped", bufs=3, align_bytes=64)
             nc.vector.tensor_copy(
-                out=ag[i, head][:].rearrange("p (c i) t -> p c t i", i=4),
-                in_=pl[i, head][:].rearrange("p t (c i) -> p c t i", i=4))
+                out=a_grouped[i, head][:].rearrange("p (c i) t -> p c t i", i=4),
+                in_=planes[i, head][:].rearrange("p t (c i) -> p c t i", i=4))
 
-        def quant_a(i, head):
-            ac[i, head] = work.tile([P, TOK], U32, name="ac", tag="ac", bufs=4, align_bytes=64)
-            asc[i, head] = work.tile([P, TOK], U8, name="asc", tag="asc", bufs=4, align_bytes=64)
+        def quantise_a(i, head):
+            a_codes[i, head] = work.tile([P, CHUNK], U32, name="a_codes", tag="a_codes", bufs=4, align_bytes=64)
+            a_scales[i, head] = work.tile([P, CHUNK], U8, name="a_scales", tag="a_scales", bufs=4, align_bytes=64)
             nc.vector.quantize_mx(
-                out=ac[i, head][:].bitcast(FP8X4), scales=asc[i, head][:],
-                in_=ag[i, head][:].rearrange("p n t -> p (n t)"))
+                out=a_codes[i, head][:].bitcast(FP8X4), scales=a_scales[i, head][:],
+                in_=a_grouped[i, head][:].rearrange("p n t -> p (n t)"))
+
 
         def second(i, head):
-            o = psum.tile([P, J, 2, LAT], F32, name="o%d" % head, tag="o%d" % head, bufs=1)
-            mm2[i, head] = o
+            result[i, head] = psum.tile([P, J, 2, LAT], F32, name="result", tag="result_%d" % head, bufs=1)
             for j in range(J):
                 cols = slice(j * P, (j + 1) * P)
                 nc.tensor.matmul_mx(
-                    out=o[:, j, :, :].rearrange("p h c -> p (h c)"),
-                    lhsT=ac[i, head][:, cols].bitcast(FP8X4), lhsT_scale=asc[i, head][:, cols],
-                    rhs=w2c[:, head, :].bitcast(FP8X4), rhs_scale=w2s[:, head, :], start=True, stop=True)
+                    out=result[i, head][:, j, :, :].rearrange("p h c -> p (h c)"),
+                    lhsT=a_codes[i, head][:, cols].bitcast(FP8X4), lhsT_scale=a_scales[i, head][:, cols],
+                    rhs=w2_codes[:, head, :].bitcast(FP8X4), rhs_scale=w2_scales[:, head, :], start=True, stop=True)
 
-        def bias(i, head):
-            if head == PRIOR:
-                v[i] = work.tile([P, 2, 2, J, LAT], F32, name="v", tag="v", bufs=8)
+        def add_bias(i, head):
             nc.vector.tensor_tensor(
-                out=v[i][:, head].rearrange("p h j c -> p j h c"),
-                in0=mm2[i, head][:],
-                in1=b2[:, head].unsqueeze(1).to_broadcast([P, J, 2, LAT]),
+                out=value[:, 2 * i + head].rearrange("p h j c -> p j h c"),
+                in0=result[i, head][:],
+                in1=bias2[:, head].unsqueeze(1).to_broadcast([P, J, 2, LAT]),
                 op=ALU.add)
             dst = prior_mean if head == PRIOR else post_mean
             nc.sync.dma_start(
-                out=dst.rearrange("(c p j) d -> c p j d", p=P, j=J)[i], in_=v[i][:, head, 0])
+                out=dst.rearrange("(c p j) d -> c p j d", p=P, j=J)[i], in_=value[:, 2 * i + head, MEAN])
 
-        def exp(i, heads=slice(0, 2)):
-            if i not in y:
-                y[i] = work.tile([P, 2, J * LAT], F32, name="y", tag="y", bufs=8)
+        def exp(e0, e1):
             nc.scalar.activation(
-                out=y[i][:, heads], in_=v[i][:, heads, 1].rearrange("p e j c -> p e (j c)"), func=ACT.Exp)
+                out=soft[:, e0:e1], in_=value[:, e0:e1, STD].rearrange("p e j c -> p e (j c)"), func=ACT.Exp)
 
-        def log(i):
-            nc.scalar.activation(out=y[i][:], in_=y[i][:], func=ACT.Ln, bias=off[:])
+        def log(e0, e1):
+            nc.scalar.activation(out=soft[:, e0:e1], in_=soft[:, e0:e1], func=ACT.Ln, bias=exp_tenth[:])
 
-        def std(i):
-            sd = v[i][:, :, 1].rearrange("p e j c -> p e (j c)")
-            nc.vector.scalar_tensor_tensor(out=sd, in0=y[i][:], scalar=LIMIT, in1=sd, op0=ALU.min, op1=ALU.max)
-            for head in HEADS:
-                dst = prior_std if head == PRIOR else post_std
+        def std(e0, e1):
+            w = value[:, e0:e1, STD].rearrange("p e j c -> p e (j c)")
+            nc.vector.scalar_tensor_tensor(
+                out=w, in0=soft[:, e0:e1], scalar=EXACT_ABOVE, in1=w, op0=ALU.min, op1=ALU.max)
+            for e in range(e0, e1):
+                dst = prior_std if e % 2 == PRIOR else post_std
                 nc.sync.dma_start(
-                    out=dst.rearrange("(c p j) d -> c p j d", p=P, j=J)[i], in_=v[i][:, head, 1])
+                    out=dst.rearrange("(c p j) d -> c p j d", p=P, j=J)[e // 2], in_=value[:, e, STD])
 
-        def spin(count):
-            for n in range(count):
-                nc.tensor.matmul(out=junk[:], lhsT=ones[:], rhs=ones[:], start=True, stop=True)
 
-        def turn_weights(src, k0, t0):
-            xt = psum.tile([P, 2, 2, P], F32, name="xt", tag="xt", bufs=2)
-            for a in (0, 1):
-                words = src[:, t0 + a, k0 : k0 + KIN].bitcast(F32)
-                for u in (0, 1):
-                    nc.tensor.transpose(xt[:, a, u, :], words[:, u : KIN // 2 : 2], ident[:])
-            return xt
-
-        def weight_dst(w, t0):
-            return w1g[:, w, t0 * P : (t0 + 2) * P, :].rearrange("p (a m) e -> p a m e", a=2).bitcast(F32)
-
-        def quant_w(w):
-            nc.vector.quantize_mx(
-                out=w1c[:, w, :].bitcast(FP8X4), scales=w1s[:, w, :],
-                in_=w1g[:, w].rearrange("p m t -> p (m t)"))
-
-        nc.vector.memset(srow[:], 0.0)
+        nc.vector.memset(scale_row[:, 0 : KIN // 2], 0.0)
+        nc.gpsimd.memset(scale_row[:, KIN // 2 : KIN], 0.0)
         nc.gpsimd.memset(ones[:], 1.0)
-        nc.vector.memset(warm[:], 0.0)
-        nc.vector.tensor_scalar(out=off[:], in0=warm[:], scalar1=math.exp(0.1), scalar2=None, op0=ALU.add)
-        nc.vector.memset(ones_b[:], 1.0)
-        nc.vector.memset(brow[:], 0.0)
+        nc.vector.memset(zero[:], 0.0)
+        nc.vector.tensor_scalar(out=exp_tenth[:], in0=zero[:], scalar1=math.exp(0.1), scalar2=None, op0=ALU.add)
+        nc.vector.memset(ones_bf16[:], 1.0)
+        nc.vector.memset(bias2_row[:], 0.0)
         make_identity(nc, ident[:])
-        nc.scalar.activation(out=warm[:], in_=warm[:], func=ACT.Exp)
+        nc.scalar.activation(out=zero[:], in_=zero[:], func=ACT.Exp)
 
-        nc.sync.dma_start(out=srow[0:1, :], in_=h_scale)
-        nc.scalar.dma_start(out=b1r[PRIOR][:], in_=bp1.rearrange("(m t) -> m t", t=4))
-        nc.scalar.dma_start(out=b1r[POST][:], in_=bq1.rearrange("(m t) -> m t", t=4))
-        nc.sync.dma_start(out=wp1r[:], in_=wp1.rearrange("(m t) k -> m t k", t=4))
+        nc.sync.dma_start(out=scale_row[0:1, :], in_=h_scale)
+        nc.scalar.dma_start(out=bias1_raw[PRIOR][:], in_=bp1.rearrange("(m t) -> m t", t=PACK))
+        nc.scalar.dma_start(out=bias1_raw[POST][:], in_=bq1.rearrange("(m t) -> m t", t=PACK))
+        nc.sync.dma_start(out=wp1_rows[:], in_=wp1.rearrange("(m t) k -> m t k", t=PACK))
         load_h(0)
-        load_e(0)
+        load_embedding(0)
         load_h(1)
-        nc.sync.dma_start(out=wq1r[:], in_=wq1.rearrange("(m t) k -> m t k", t=4))
-        load_e(1)
+        nc.sync.dma_start(out=wq1_rows[:], in_=wq1.rearrange("(m t) k -> m t k", t=PACK))
+        load_embedding(1)
         load_h(2)
-        nc.sync.dma_start(out=w2r[:, PRIOR, :], in_=wp2)
-        nc.sync.dma_start(out=w2r[:, POST, :], in_=wq2)
-        nc.sync.dma_start(out=brow[0:1, 0:DIST], in_=bp2.unsqueeze(0))
-        nc.sync.dma_start(out=brow[0:1, DIST : 2 * DIST], in_=bq2.unsqueeze(0))
-        load_e(2)
+        nc.sync.dma_start(out=w2_rows[:, PRIOR, :], in_=wp2)
+        nc.sync.dma_start(out=w2_rows[:, POST, :], in_=wq2)
+        nc.sync.dma_start(out=bias2_row[0:1, 0:DIST], in_=bp2.unsqueeze(0))
+        nc.sync.dma_start(out=bias2_row[0:1, DIST : 2 * DIST], in_=bq2.unsqueeze(0))
+        load_embedding(2)
         load_h(3)
-        load_e(3)
+        load_embedding(3)
         load_h(4)
-        load_e(4)
+        load_embedding(4)
 
         with tc.manual_schedule(engines={ENG.PE, ENG.Activation, ENG.DVE}):
-            junk = psum.tile([P, P], F32, name="o1", tag="o1", bufs=1)
-            spin(5)
-            sp = psum.tile([P, KIN], F32, name="o0", tag="o0", bufs=1)
-            nc.tensor.matmul(out=sp[:], lhsT=ones[:], rhs=srow[:], start=True, stop=True)
-            nc.scalar.copy(out=scale[:], in_=sp[:])
-            x = turn_weights(wp1r, 0, 0)
-            nc.scalar.copy(out=weight_dst(0, 0), in_=x[:].rearrange("p a u m -> p a m u"))
-            x = turn_weights(wp1r, 0, 2)
-            nc.scalar.copy(out=weight_dst(0, 2), in_=x[:].rearrange("p a u m -> p a m u"))
+            unread = psum.tile([P, P], F32, name="unread", tag="result_1", bufs=1)
+            filler(6)
+            for half, tag, count in ((0, "result_0", 1), (1, "acc", 4)):
+                cols = slice(half * KIN // 2, (half + 1) * KIN // 2)
+                spread = psum.tile([P, KIN // 2], F32, name="spread", tag=tag, bufs=count)
+                nc.tensor.matmul(out=spread[:], lhsT=ones[:], rhs=scale_row[:, cols], start=True, stop=True)
+                nc.scalar.copy(out=scale[:, 0, cols], in_=spread[:])
+            for t0 in (0, 2):
+                unload_weights(nc.scalar.copy, 0, t0, turn_weights(wp1_rows, 0, t0))
             widen(0)
-            spin(2)
-            quant_w(0)
-            unload(0, 0, turn(0, 0))
-            unload(0, 1, turn(0, 1))
-            spin(2)
-            unload(0, 2, turn(0, 2))
-            unload(0, 3, turn(0, 3))
+            filler(2)
+            quantise_weights(0)
+            turn(0, 0)
+            filler(2)
+            turn(0, 1)
+            turn(0, 2)
+            filler(1)
+            turn(0, 3)
             load_h(5)
-            load_e(5)
-            widen(1)
+            load_embedding(5)
+            filler(1)
+            unload_weights(nc.scalar.copy, 1, 0, turn_weights(wq1_rows, 0, 0))
+            nc.scalar.copy(out=scale[:, 1], in_=scale[:, 0])
+            filler(2)
+            unload_weights(nc.scalar.copy, 1, 2, turn_weights(wq1_rows, 0, 2))
             for head in HEADS:
-                nc.vector.tensor_copy(out=b1[head][:], in_=b1r[head][:])
-            spin(2)
-            x = turn_weights(wq1r, 0, 0)
-            nc.scalar.copy(out=weight_dst(1, 0), in_=x[:].rearrange("p a u m -> p a m u"))
-            x = turn_weights(wq1r, 0, 2)
-            nc.scalar.copy(out=weight_dst(1, 2), in_=x[:].rearrange("p a u m -> p a m u"))
-            quant_c(0)
-            spin(1)
-            quant_w(1)
-            x = turn_weights(wq1r, 512, 2)
-            nc.scalar.copy(out=weight_dst(2, 2), in_=x[:].rearrange("p a u m -> p a m u"))
+                nc.vector.tensor_copy(out=bias1[head][:], in_=bias1_raw[head][:])
+            widen(1)
+            quantise_c(0)
+            quantise_weights(1)
+            unload_weights(nc.vector.tensor_copy, 2, 2, turn_weights(wq1_rows, KIN, 2))
             first(0, PRIOR)
-            x = turn_weights(wq1r, 512, 0)
-            nc.vector.tensor_copy(out=weight_dst(2, 0), in_=x[:].rearrange("p a u m -> p a m u"))
-            unload(1, 0, turn(1, 0))
-            unload(1, 1, turn(1, 1))
-            unload(1, 2, turn(1, 2))
-            spin(2)
-            unload(1, 3, turn(1, 3))
+            turn(1, 0)
+            unload_weights(nc.scalar.copy, 2, 0, turn_weights(wq1_rows, KIN, 0))
+            filler(2)
+            turn(1, 1)
+            filler(1)
+            turn(1, 2)
+            turn(1, 3)
             widen(2)
-            quant_w(2)
+            quantise_weights(2)
             first(0, POST)
             interleave(0, PRIOR)
+            quantise_c(1)
+            turn(2, 0)
+            turn(2, 1)
+            filler(1)
+            quantise_a(0, PRIOR)
+            turn(2, 2)
             widen(3)
-            quant_a(0, PRIOR)
-            quant_c(1)
-            unload(2, 0, turn(2, 0))
-            unload(2, 1, turn(2, 1))
-            spin(1)
-            unload(2, 2, turn(2, 2))
-            unload(2, 3, turn(2, 3))
-            quant_c(2)
-            spin(2)
-            x = psum.tile([P, 2, 2, P], F32, name="xt", tag="xt", bufs=2)
+            turn(2, 3)
+            filler(2)
+            quantise_c(2)
+            bank = psum.tile([P, 2, 2, P], F32, name="turned", tag="turned", bufs=2)
             for head in HEADS:
-                words = w2r[:, head, :].bitcast(F32)
+                words = w2_rows[:, head, :].bitcast(F32)
                 for u in (0, 1):
-                    nc.tensor.transpose(x[:, head, u, :], words[:, u : KIN // 2 : 2], ident[:])
-            nc.scalar.copy(out=w2g[:].bitcast(F32), in_=x[:].rearrange("p a u m -> p a m u"))
-            bp = psum.tile([P, 2, 2, LAT], F32, name="o1", tag="o1", bufs=1)
-            nc.tensor.matmul(out=bp[:].rearrange("p e h c -> p (e h c)"), lhsT=ones_b[:], rhs=brow[:], start=True, stop=True)
+                    nc.tensor.transpose(bank[:, head, u, :], words[:, u : KIN // 2 : 2], ident[:])
+            nc.scalar.copy(out=w2_grouped[:].bitcast(F32), in_=bank[:].rearrange("p a u m -> p a m u"))
+            spread2 = psum.tile([P, 2, 2, LAT], F32, name="spread2", tag="result_1", bufs=1)
+            nc.tensor.matmul(
+                out=spread2[:].rearrange("p e h c -> p (e h c)"), lhsT=ones_bf16[:], rhs=bias2_row[:], start=True, stop=True)
             nc.vector.quantize_mx(
-                out=w2c[:].rearrange("p e m -> p (e m)").bitcast(FP8X4),
-                scales=w2s[:].rearrange("p e m -> p (e m)"),
-                in_=w2g[:].rearrange("p e m t -> p (e m t)"))
-            nc.vector.tensor_copy(out=b2[:, :, 0], in_=bp[:, :, 0])
-            nc.vector.tensor_scalar(out=b2[:, :, 1], in0=bp[:, :, 1], scalar1=0.1, scalar2=None, op0=ALU.add)
-
-            def has(c):
-                return 0 <= c < CHUNKS
+                out=w2_codes[:].rearrange("p e m -> p (e m)").bitcast(FP8X4),
+                scales=w2_scales[:].rearrange("p e m -> p (e m)"),
+                in_=w2_grouped[:].rearrange("p e m t -> p (e m t)"))
+            nc.vector.tensor_copy(out=bias2[:, :, MEAN], in_=spread2[:, :, MEAN])
+            nc.vector.tensor_scalar(out=bias2[:, :, STD], in0=spread2[:, :, STD], scalar1=0.1, scalar2=None, op0=ALU.add)
 
             for i in range(1, CHUNKS - 1):
-                n = i + 2
-                if has(n + 3) and n + 3 > 3:
-                    load_h(n + 3)
-                    load_e(n + 3)
-                if has(n):
-                    for j in (0, 1):
-                        unload(n, j, turn(n, j))
-                if has(i - 1):
-                    interleave(i - 1, POST)
-                if has(i):
-                    first(i, PRIOR)
-                if has(i - 2):
-                    second(i - 2, PRIOR)
-                    second(i - 2, POST)
-                if has(i - 3):
-                    exp(i - 3)
-                if has(n):
-                    for j in (2, 3):
-                        unload(n, j, turn(n, j))
-                if has(n + 1):
-                    widen(n + 1)
-                if has(i - 1):
-                    quant_a(i - 1, POST)
-                if has(i - 2):
-                    bias(i - 2, PRIOR)
-                    bias(i - 2, POST)
-                if has(i):
-                    first(i, POST)
-                    interleave(i, PRIOR)
-                if has(n):
-                    quant_c(n)
-                if has(i):
-                    quant_a(i, PRIOR)
+                turning = i + 2 < CHUNKS
+                if i + 5 < CHUNKS:
+                    load_h(i + 5)
+                    load_embedding(i + 5)
+                if turning:
+                    turn(i + 2, 0)
+                    turn(i + 2, 1)
+                interleave(i - 1, POST)
+                first(i, PRIOR)
+                if i >= 2:
+                    for head in HEADS:
+                        second(i - 2, head)
+                if i >= 3:
+                    exp(2 * (i - 3), 2 * (i - 2))
+                if turning:
+                    turn(i + 2, 2)
+                    turn(i + 2, 3)
+                if i + 3 < CHUNKS:
+                    widen(i + 3)
+                if i >= 2:
+                    for head in HEADS:
+                        add_bias(i - 2, head)
+                quantise_a(i - 1, POST)
+                first(i, POST)
+                interleave(i, PRIOR)
+                if turning:
+                    quantise_c(i + 2)
+                quantise_a(i, PRIOR)
 
-            i = CHUNKS - 1
-            first(i, PRIOR)
-            second(i - 2, PRIOR)
-            second(i - 2, POST)
-            exp(i - 3)
-            interleave(i - 1, POST)
-            bias(i - 2, PRIOR)
-            bias(i - 2, POST)
-            quant_a(i - 1, POST)
-            first(i, POST)
-            exp(i - 2)
-            for c in range(i - 1):
-                log(c)
-            interleave(i, PRIOR)
-            second(i - 1, PRIOR)
-            second(i - 1, POST)
-            quant_a(i, PRIOR)
-            bias(i - 1, PRIOR)
-            bias(i - 1, POST)
-            exp(i - 1)
-            interleave(i, POST)
-            second(i, PRIOR)
-            bias(i, PRIOR)
-            exp(i, slice(0, 1))
-            quant_a(i, POST)
-            for c in range(i - 1):
-                std(c)
-                if c == 0:
-                    second(i, POST)
-                    bias(i, POST)
-                    exp(i, slice(1, 2))
-            for c in (i - 1, i):
-                log(c)
-                std(c)
+            last = CHUNKS - 1
+            early = 2 * (last - 1)
+            first(last, PRIOR)
+            for head in HEADS:
+                second(last - 2, head)
+            exp(2 * (last - 3), 2 * (last - 2))
+            interleave(last - 1, POST)
+            for head in HEADS:
+                add_bias(last - 2, head)
+            quantise_a(last - 1, POST)
+            first(last, POST)
+            exp(2 * (last - 2), 2 * (last - 1))
+            for e in range(0, early, 4):
+                log(e, e + 4)
+            interleave(last, PRIOR)
+            for head in HEADS:
+                second(last - 1, head)
+            add_bias(last - 1, PRIOR)
+            quantise_a(last, PRIOR)
+            add_bias(last - 1, POST)
+            exp(2 * (last - 1), 2 * last)
+            interleave(last, POST)
+            second(last, PRIOR)
+            add_bias(last, PRIOR)
+            exp(2 * last, 2 * last + 1)
+            quantise_a(last, POST)
+            std(0, 4)
+            second(last, POST)
+            add_bias(last, POST)
+            exp(2 * last + 1, 2 * last + 2)
+            for e in range(4, early, 4):
+                std(e, e + 4)
+            for e in (early, early + 2):
+                log(e, e + 2)
+                std(e, e + 2)

import math
from contextlib import ExitStack

import concourse.mybir as mybir
from concourse.masks import make_identity

B, KIN, HID, DIST, LAT = 4096, 512, 512, 128, 64
FLOPS = 2 * B * (HID * KIN + HID * 2 * KIN + 2 * DIST * HID)

P = 128
J = 4
PACK = 4
CHUNK = P * J
CHUNKS = B // CHUNK

F32 = mybir.dt.float32
BF16 = mybir.dt.bfloat16
U32 = mybir.dt.uint32
U8 = mybir.dt.uint8
FP8 = mybir.dt.float8_e4m3fn
FP8X4 = mybir.dt.float8_e4m3fn_x4
ACT = mybir.ActivationFunctionType
ALU = mybir.AluOpType
ENG = mybir.EngineType

EXACT_ABOVE = 40.0
PRIOR, POST = 0, 1
HEADS = (PRIOR, POST)
MEAN, STD = 0, 1
PASSES = {PRIOR: ((0, 0),), POST: ((1, 0), (2, 1))}


def tile_rssmcell_pb_t_kernel(
    tc, h_bytes, h_scale, embedding, wp1, bp1, wp2, bp2, wq1, bq1, wq2, bq2,
    post_mean, post_std, prior_mean, prior_std,
):
    nc = tc.nc
    with ExitStack() as ctx:
        keep = ctx.enter_context(tc.tile_pool(name="keep", bufs=1))
        work = ctx.enter_context(tc.tile_pool(name="work", bufs=2))
        psum = ctx.enter_context(tc.psum_pool(name="psum", bufs=1))

        scale_row = keep.tile([P, KIN], F32, name="scale_row", tag="scale_row")
        bias2_row = keep.tile([P, 2 * DIST], BF16, name="bias2_row", tag="bias2_row")
        ones = keep.tile([P, P], F32, name="ones", tag="ones")
        ones_bf16 = keep.tile([P, P], BF16, name="ones_bf16", tag="ones_bf16")
        ident = keep.tile([P, P], F32, name="ident", tag="ident")
        zero = keep.tile([P, 1], F32, name="zero", tag="zero")
        bias1_raw = [keep.tile([P, PACK], BF16, name="bias1_raw_%d" % e, tag="bias1_raw_%d" % e) for e in HEADS]
        bias1 = [keep.tile([P, PACK], F32, name="bias1_%d" % e, tag="bias1_%d" % e) for e in HEADS]
        bias2 = keep.tile([P, 2, 2, LAT], F32, name="bias2", tag="bias2")
        scale = keep.tile([P, 2, KIN], F32, name="scale", tag="scale", align_bytes=64)
        exp_tenth = keep.tile([P, 1], F32, name="exp_tenth", tag="exp_tenth")
        wp1_rows = keep.tile([P, PACK, KIN], BF16, name="wp1_rows", tag="wp1_rows")
        wq1_rows = keep.tile([P, PACK, 2 * KIN], BF16, name="wq1_rows", tag="wq1_rows")
        w2_rows = keep.tile([P, 2, HID], BF16, name="w2_rows", tag="w2_rows")
        value = keep.tile([P, 2 * CHUNKS, 2, J, LAT], F32, name="value", tag="value")
        soft = keep.tile([P, 2 * CHUNKS, J * LAT], F32, name="soft", tag="soft")
        w1_grouped = keep.tile([P, 3, HID, PACK], BF16, name="w1_grouped", tag="w1_grouped", align_bytes=64)
        w1_codes = keep.tile([P, 3, HID], U32, name="w1_codes", tag="w1_codes", align_bytes=64)
        w1_scales = keep.tile([P, 3, HID], U8, name="w1_scales", tag="w1_scales", align_bytes=64)
        w2_grouped = keep.tile([P, 2, DIST, PACK], BF16, name="w2_grouped", tag="w2_grouped", align_bytes=64)
        w2_codes = keep.tile([P, 2, DIST], U32, name="w2_codes", tag="w2_codes", align_bytes=64)
        w2_scales = keep.tile([P, 2, DIST], U8, name="w2_scales", tag="w2_scales", align_bytes=64)

        h_raw, emb, h_wide, c_grouped, c_codes, c_scales = {}, {}, {}, {}, {}, {}
        planes, a_grouped, a_codes, a_scales, result = {}, {}, {}, {}, {}


        def turn_weights(rows, k0, t0):
            bank = psum.tile([P, 2, 2, P], F32, name="turned", tag="turned", bufs=2)
            for a in (0, 1):
                words = rows[:, t0 + a, k0 : k0 + KIN].bitcast(F32)
                for u in (0, 1):
                    nc.tensor.transpose(bank[:, a, u, :], words[:, u : KIN // 2 : 2], ident[:])
            return bank

        def unload_weights(copy, w, t0, bank):
            dst = w1_grouped[:, w, t0 * P : (t0 + 2) * P, :].rearrange("p (a m) e -> p a m e", a=2).bitcast(F32)
            copy(out=dst, in_=bank[:].rearrange("p a u m -> p a m u"))

        def quantise_weights(w):
            nc.vector.quantize_mx(
                out=w1_codes[:, w, :].bitcast(FP8X4), scales=w1_scales[:, w, :],
                in_=w1_grouped[:, w].rearrange("p m t -> p (m t)"))

        def filler(count):
            for n in range(count):
                nc.tensor.matmul(out=unread[:], lhsT=ones[:], rhs=ones[:], start=True, stop=True)


        def load_h(i):
            h_raw[i] = work.tile([P, J, KIN], U8, name="h_raw", tag="h_raw", bufs=5, align_bytes=64)
            nc.sync.dma_start(out=h_raw[i][:], in_=h_bytes.rearrange("(c p j) k -> c p j k", p=P, j=J)[i])

        def load_embedding(i):
            emb[i] = work.tile([P, J, KIN], BF16, name="emb", tag="emb", bufs=5)
            nc.sync.dma_start(out=emb[i][:], in_=embedding.rearrange("(c p j) k -> c p j k", p=P, j=J)[i])

        def widen(i):
            h_wide[i] = work.tile([P, J, KIN], BF16, name="h_wide", tag="h_wide", bufs=3, align_bytes=64)
            step = 1 if i < 2 else 2
            for j in range(0, J, step):
                rows = slice(j, j + step)
                nc.vector.tensor_tensor(
                    out=h_wide[i][:, rows].rearrange("p j k -> p (j k)"),
                    in0=h_raw[i][:, rows].rearrange("p j k -> p (j k)").bitcast(FP8),
                    in1=scale[:, 0:step].rearrange("p j k -> p (j k)"), op=ALU.mult)

        def turn(i, j):
            bank = psum.tile([P, 2, 2, P], F32, name="turned", tag="turned", bufs=2)
            for g, rows in enumerate((h_wide[i], emb[i])):
                words = rows[:, j, :].bitcast(F32)
                for u in (0, 1):
                    nc.tensor.transpose(bank[:, g, u, :], words[:, u : KIN // 2 : 2], ident[:])
            if j == 0:
                c_grouped[i] = work.tile([P, 2, CHUNK, PACK], BF16, name="c_grouped", tag="c_grouped", bufs=2, align_bytes=64)
            dst = c_grouped[i][:, :, j * P : (j + 1) * P, :].bitcast(F32)
            nc.scalar.copy(out=dst, in_=bank[:].rearrange("p g u r -> p g r u"))

        def quantise_c(i):
            c_codes[i] = work.tile([P, 2, CHUNK], U32, name="c_codes", tag="c_codes", bufs=3, align_bytes=64)
            c_scales[i] = work.tile([P, 2, CHUNK], U8, name="c_scales", tag="c_scales", bufs=3, align_bytes=64)
            step = 1 if i == 0 else 2
            for g in range(0, 2, step):
                part = slice(g, g + step)
                nc.vector.quantize_mx(
                    out=c_codes[i][:, part].rearrange("p g n -> p (g n)").bitcast(FP8X4),
                    scales=c_scales[i][:, part].rearrange("p g n -> p (g n)"),
                    in_=c_grouped[i][:, part].rearrange("p g n t -> p (g n t)"))


        def first(i, head):
            planes[i, head] = work.tile([P, PACK, CHUNK], BF16, name="planes", tag="planes", bufs=3, align_bytes=64)
            passes = PASSES[head]
            for t in range(PACK):
                acc = psum.tile([P, CHUNK], F32, name="acc", tag="acc", bufs=4)
                cols = slice(t * P, (t + 1) * P)
                for n, (w, g) in enumerate(passes):
                    nc.tensor.matmul_mx(
                        out=acc[:], lhsT=w1_codes[:, w, cols].bitcast(FP8X4), lhsT_scale=w1_scales[:, w, cols],
                        rhs=c_codes[i][:, g, :].bitcast(FP8X4), rhs_scale=c_scales[i][:, g, :],
                        start=(n == 0), stop=(n == len(passes) - 1))
                dst = planes[i, head][:, t, :]
                bias = bias1[head][:, t : t + 1]
                if (i, head, t) == (0, PRIOR, 2):
                    nc.vector.tensor_scalar(out=dst, in0=acc[:], scalar1=bias, scalar2=0.0, op0=ALU.add, op1=ALU.max)
                else:
                    nc.scalar.activation(out=dst, in_=acc[:], func=ACT.Relu, bias=bias)

        def interleave(i, head):
            a_grouped[i, head] = work.tile([P, CHUNK, PACK], BF16, name="a_grouped", tag="a_grouped", bufs=3, align_bytes=64)
            nc.vector.tensor_copy(
                out=a_grouped[i, head][:].rearrange("p (c i) t -> p c t i", i=4),
                in_=planes[i, head][:].rearrange("p t (c i) -> p c t i", i=4))

        def quantise_a(i, head):
            a_codes[i, head] = work.tile([P, CHUNK], U32, name="a_codes", tag="a_codes", bufs=4, align_bytes=64)
            a_scales[i, head] = work.tile([P, CHUNK], U8, name="a_scales", tag="a_scales", bufs=4, align_bytes=64)
            nc.vector.quantize_mx(
                out=a_codes[i, head][:].bitcast(FP8X4), scales=a_scales[i, head][:],
                in_=a_grouped[i, head][:].rearrange("p n t -> p (n t)"))


        def second(i, head):
            result[i, head] = psum.tile([P, J, 2, LAT], F32, name="result", tag="result_%d" % head, bufs=1)
            for j in range(J):
                cols = slice(j * P, (j + 1) * P)
                nc.tensor.matmul_mx(
                    out=result[i, head][:, j, :, :].rearrange("p h c -> p (h c)"),
                    lhsT=a_codes[i, head][:, cols].bitcast(FP8X4), lhsT_scale=a_scales[i, head][:, cols],
                    rhs=w2_codes[:, head, :].bitcast(FP8X4), rhs_scale=w2_scales[:, head, :], start=True, stop=True)

        def add_bias(i, head):
            nc.vector.tensor_tensor(
                out=value[:, 2 * i + head].rearrange("p h j c -> p j h c"),
                in0=result[i, head][:],
                in1=bias2[:, head].unsqueeze(1).to_broadcast([P, J, 2, LAT]),
                op=ALU.add)
            dst = prior_mean if head == PRIOR else post_mean
            nc.sync.dma_start(
                out=dst.rearrange("(c p j) d -> c p j d", p=P, j=J)[i], in_=value[:, 2 * i + head, MEAN])

        def exp(e0, e1):
            nc.scalar.activation(
                out=soft[:, e0:e1], in_=value[:, e0:e1, STD].rearrange("p e j c -> p e (j c)"), func=ACT.Exp)

        def log(e0, e1):
            nc.scalar.activation(out=soft[:, e0:e1], in_=soft[:, e0:e1], func=ACT.Ln, bias=exp_tenth[:])

        def std(e0, e1):
            w = value[:, e0:e1, STD].rearrange("p e j c -> p e (j c)")
            nc.vector.scalar_tensor_tensor(
                out=w, in0=soft[:, e0:e1], scalar=EXACT_ABOVE, in1=w, op0=ALU.min, op1=ALU.max)
            for e in range(e0, e1):
                dst = prior_std if e % 2 == PRIOR else post_std
                nc.sync.dma_start(
                    out=dst.rearrange("(c p j) d -> c p j d", p=P, j=J)[e // 2], in_=value[:, e, STD])


        nc.vector.memset(scale_row[:, 0 : KIN // 2], 0.0)
        nc.gpsimd.memset(scale_row[:, KIN // 2 : KIN], 0.0)
        nc.gpsimd.memset(ones[:], 1.0)
        nc.vector.memset(zero[:], 0.0)
        nc.vector.tensor_scalar(out=exp_tenth[:], in0=zero[:], scalar1=math.exp(0.1), scalar2=None, op0=ALU.add)
        nc.vector.memset(ones_bf16[:], 1.0)
        nc.vector.memset(bias2_row[:], 0.0)
        make_identity(nc, ident[:])
        nc.scalar.activation(out=zero[:], in_=zero[:], func=ACT.Exp)

        nc.sync.dma_start(out=scale_row[0:1, :], in_=h_scale)
        nc.scalar.dma_start(out=bias1_raw[PRIOR][:], in_=bp1.rearrange("(m t) -> m t", t=PACK))
        nc.scalar.dma_start(out=bias1_raw[POST][:], in_=bq1.rearrange("(m t) -> m t", t=PACK))
        nc.sync.dma_start(out=wp1_rows[:], in_=wp1.rearrange("(m t) k -> m t k", t=PACK))
        load_h(0)
        load_embedding(0)
        load_h(1)
        nc.sync.dma_start(out=wq1_rows[:], in_=wq1.rearrange("(m t) k -> m t k", t=PACK))
        load_embedding(1)
        load_h(2)
        nc.sync.dma_start(out=w2_rows[:, PRIOR, :], in_=wp2)
        nc.sync.dma_start(out=w2_rows[:, POST, :], in_=wq2)
        nc.sync.dma_start(out=bias2_row[0:1, 0:DIST], in_=bp2.unsqueeze(0))
        nc.sync.dma_start(out=bias2_row[0:1, DIST : 2 * DIST], in_=bq2.unsqueeze(0))
        load_embedding(2)
        load_h(3)
        load_embedding(3)
        load_h(4)
        load_embedding(4)

        with tc.manual_schedule(engines={ENG.PE, ENG.Activation, ENG.DVE}):
            unread = psum.tile([P, P], F32, name="unread", tag="result_1", bufs=1)
            filler(6)
            for half, tag, count in ((0, "result_0", 1), (1, "acc", 4)):
                cols = slice(half * KIN // 2, (half + 1) * KIN // 2)
                spread = psum.tile([P, KIN // 2], F32, name="spread", tag=tag, bufs=count)
                nc.tensor.matmul(out=spread[:], lhsT=ones[:], rhs=scale_row[:, cols], start=True, stop=True)
                nc.scalar.copy(out=scale[:, 0, cols], in_=spread[:])
            for t0 in (0, 2):
                unload_weights(nc.scalar.copy, 0, t0, turn_weights(wp1_rows, 0, t0))
            widen(0)
            filler(2)
            quantise_weights(0)
            turn(0, 0)
            filler(2)
            turn(0, 1)
            turn(0, 2)
            filler(1)
            turn(0, 3)
            load_h(5)
            load_embedding(5)
            filler(1)
            unload_weights(nc.scalar.copy, 1, 0, turn_weights(wq1_rows, 0, 0))
            nc.scalar.copy(out=scale[:, 1], in_=scale[:, 0])
            filler(2)
            unload_weights(nc.scalar.copy, 1, 2, turn_weights(wq1_rows, 0, 2))
            for head in HEADS:
                nc.vector.tensor_copy(out=bias1[head][:], in_=bias1_raw[head][:])
            widen(1)
            quantise_c(0)
            quantise_weights(1)
            unload_weights(nc.vector.tensor_copy, 2, 2, turn_weights(wq1_rows, KIN, 2))
            first(0, PRIOR)
            turn(1, 0)
            unload_weights(nc.scalar.copy, 2, 0, turn_weights(wq1_rows, KIN, 0))
            filler(2)
            turn(1, 1)
            filler(1)
            turn(1, 2)
            turn(1, 3)
            widen(2)
            quantise_weights(2)
            first(0, POST)
            interleave(0, PRIOR)
            quantise_c(1)
            turn(2, 0)
            turn(2, 1)
            filler(1)
            quantise_a(0, PRIOR)
            turn(2, 2)
            widen(3)
            turn(2, 3)
            filler(2)
            quantise_c(2)
            bank = psum.tile([P, 2, 2, P], F32, name="turned", tag="turned", bufs=2)
            for head in HEADS:
                words = w2_rows[:, head, :].bitcast(F32)
                for u in (0, 1):
                    nc.tensor.transpose(bank[:, head, u, :], words[:, u : KIN // 2 : 2], ident[:])
            nc.scalar.copy(out=w2_grouped[:].bitcast(F32), in_=bank[:].rearrange("p a u m -> p a m u"))
            spread2 = psum.tile([P, 2, 2, LAT], F32, name="spread2", tag="result_1", bufs=1)
            nc.tensor.matmul(
                out=spread2[:].rearrange("p e h c -> p (e h c)"), lhsT=ones_bf16[:], rhs=bias2_row[:], start=True, stop=True)
            nc.vector.quantize_mx(
                out=w2_codes[:].rearrange("p e m -> p (e m)").bitcast(FP8X4),
                scales=w2_scales[:].rearrange("p e m -> p (e m)"),
                in_=w2_grouped[:].rearrange("p e m t -> p (e m t)"))
            nc.vector.tensor_copy(out=bias2[:, :, MEAN], in_=spread2[:, :, MEAN])
            nc.vector.tensor_scalar(out=bias2[:, :, STD], in0=spread2[:, :, STD], scalar1=0.1, scalar2=None, op0=ALU.add)

            for i in range(1, CHUNKS - 1):
                turning = i + 2 < CHUNKS
                if i + 5 < CHUNKS:
                    load_h(i + 5)
                    load_embedding(i + 5)
                if turning:
                    turn(i + 2, 0)
                    turn(i + 2, 1)
                interleave(i - 1, POST)
                first(i, PRIOR)
                if i >= 2:
                    for head in HEADS:
                        second(i - 2, head)
                if i >= 3:
                    exp(2 * (i - 3), 2 * (i - 2))
                if turning:
                    turn(i + 2, 2)
                    turn(i + 2, 3)
                if i + 3 < CHUNKS:
                    widen(i + 3)
                if i >= 2:
                    for head in HEADS:
                        add_bias(i - 2, head)
                quantise_a(i - 1, POST)
                first(i, POST)
                interleave(i, PRIOR)
                if turning:
                    quantise_c(i + 2)
                quantise_a(i, PRIOR)

            last = CHUNKS - 1
            early = 2 * (last - 1)
            first(last, PRIOR)
            for head in HEADS:
                second(last - 2, head)
            exp(2 * (last - 3), 2 * (last - 2))
            interleave(last - 1, POST)
            for head in HEADS:
                add_bias(last - 2, head)
            quantise_a(last - 1, POST)
            first(last, POST)
            exp(2 * (last - 2), 2 * (last - 1))
            for e in range(0, early, 4):
                log(e, e + 4)
            interleave(last, PRIOR)
            for head in HEADS:
                second(last - 1, head)
            add_bias(last - 1, PRIOR)
            quantise_a(last, PRIOR)
            add_bias(last - 1, POST)
            exp(2 * (last - 1), 2 * last)
            interleave(last, POST)
            second(last, PRIOR)
            add_bias(last, PRIOR)
            exp(2 * last, 2 * last + 1)
            quantise_a(last, POST)
            std(0, 4)
            second(last, POST)
            add_bias(last, POST)
            exp(2 * last + 1, 2 * last + 2)
            for e in range(4, early, 4):
                std(e, e + 4)
            for e in (early, early + 2):
                log(e, e + 2)
                std(e, e + 2)
